import numpy as np
import ml_dtypes


def mxq(x, axis, fmt="e4m3"):
    dtype, down = {"e4m3": (ml_dtypes.float8_e4m3fn, 7), "e5m2": (ml_dtypes.float8_e5m2, 14)}[fmt]
    v = np.moveaxis(np.asarray(x, np.float32).astype(ml_dtypes.bfloat16).astype(np.float64), axis, -1)
    blocks = v.reshape(v.shape[:-1] + (-1, 32))
    amax = np.abs(blocks).max(-1, keepdims=True)
    byte = np.maximum(np.where(amax > 0, np.frexp(amax)[1] - 1 + 127, 0) - down, 1)
    scale = np.exp2(byte - 127.0)
    codes = (blocks / scale).astype(np.float32).astype(dtype).astype(np.float64)
    return np.moveaxis((codes * scale).reshape(v.shape), -1, axis)


WIDE = False


def mx_kscale(k):
    if not WIDE:
        return np.ones(k)
    levels = np.array([10, -10, 5, -5, 0])
    a = np.random.permutation(np.resize(levels, k // 512 * 4)).reshape(k // 512, 4)
    idx = np.arange(k)
    return np.exp2(a[idx // 512, idx % 128 // 32])


BF16 = ml_dtypes.bfloat16


def bf(x):
    return np.asarray(x, np.float32).astype(BF16)


def f64(x):
    return np.asarray(x).astype(np.float64)


E2M1 = np.array([0.0, 0.5, 1.0, 1.5, 2.0, 3.0, 4.0, 6.0, -0.0, -0.5, -1.0, -1.5, -2.0, -3.0, -4.0, -6.0])


def pack_weight(w, fmt):
    k, n = w.shape
    w = f64(bf(w)).reshape(k // 32, 32, n)
    amax = np.abs(w).max(1)
    if fmt == "e4m3":
        byte = np.frexp(amax)[1] - 1 + 127 - 7
    else:
        mant, ex = np.frexp(amax / 6.0)
        byte = np.where(mant > 0.5, ex, ex - 1) + 127
    byte = np.clip(np.where(amax > 0, byte, 1), 1, 254)
    scaled = (w * np.exp2(127.0 - byte)[:, None, :]).reshape(k, n).astype(np.float32)
    by_word = np.ascontiguousarray(scaled.reshape(k // 512, 128, 4, n).transpose(0, 1, 3, 2))
    if fmt == "e4m3":
        words = by_word.astype(ml_dtypes.float8_e4m3fn).view(np.uint8)
    else:
        c = by_word.astype(ml_dtypes.float4_e2m1fn).view(np.uint8) & 0xF
        words = c[..., 0::2] | (c[..., 1::2] << 4)
    return np.ascontiguousarray(words), np.ascontiguousarray(byte.astype(np.uint8).reshape(k // 512, 16, n))


def unpack_weight(words, scales, fmt):
    g, p, n, _ = words.shape
    if fmt == "e4m3":
        vals = np.ascontiguousarray(words).view(ml_dtypes.float8_e4m3fn).astype(np.float64)
    else:
        nib = np.empty((g, p, n, 4), np.uint8)
        nib[..., 0::2] = words & 0xF
        nib[..., 1::2] = words >> 4
        vals = E2M1[nib]
    vals = vals * np.repeat(np.exp2(scales.astype(np.float64) - 127.0), 8, axis=1)[..., None]
    return vals.transpose(0, 1, 3, 2).reshape(g * 512, n)


B, T, D, H = 128, 32, 1024, 1
NEG_INF = -1e30


def setup_inputs():
    s = mx_kscale(D)
    h = bf(np.random.standard_normal((B, T, D)) * s)
    stack = np.random.standard_normal((H, D, D)) * 3.0 / D / s[:, None] / s[None, :]
    words, scales = pack_weight(stack.reshape(-1, D), "e4m3")
    return {"h": h, "A_words": words, "A_scales": scales}


def reference(h, A_words, A_scales):
    hq = mxq(f64(h), 2, "e4m3")
    Aq = unpack_weight(A_words, A_scales, "e4m3").reshape(H, D, D)
    hA = hq[:, None, 1:] @ Aq[None]
    rest = mxq(hA, 3, "e4m3") @ hq[:, None].transpose(0, 1, 3, 2)
    scores = np.concatenate([np.zeros((B, H, 1, T)), rest], axis=2)
    causal = np.tril(np.ones((T, T), dtype=bool))
    scores = np.where(causal, scores, NEG_INF)
    e = np.exp(scores - scores.max(-1, keepdims=True))
    return e / e.sum(-1, keepdims=True)

@@ -1,0 +1,194 @@
+from contextlib import ExitStack
+
+import concourse.mybir as mybir
+from concourse.masks import make_identity
+
+F32 = mybir.dt.float32
+BF16 = mybir.dt.bfloat16
+I32 = mybir.dt.int32
+U32 = mybir.dt.uint32
+U8 = mybir.dt.uint8
+FP8X4 = mybir.dt.float8_e4m3fn_x4
+ALU = mybir.AluOpType
+EXP = mybir.ActivationFunctionType.Exp
+LAST_AXIS = mybir.AxisListType.X
+
+P = 128
+PACK = 4
+K_PASS = P * PACK
+SEQS, T, D = 128, 32, 1024
+PASSES = D // K_PASS
+CHUNK = P
+SEQS_IN_CHUNK = CHUNK // T
+ROUND = 2
+N_ROUNDS = SEQS * T // (CHUNK * ROUND)
+QUAD = 4
+ROUNDS_IN_QUAD = QUAD // ROUND
+NEG_INF = -1e30
+SCALAR_TAKES_EVERY = 4
+
+FLOPS = 2 * SEQS * (T - 1) * D * D + 2 * SEQS * (T - 1) * T * D
+
+
+def tile_causalselfattention_pa_t_e_kernel(tc, h, A_words, A_scales, out):
+    nc = tc.nc
+    with ExitStack() as stack:
+        const = stack.enter_context(tc.tile_pool(name="const", bufs=1))
+        h_pool = stack.enter_context(tc.tile_pool(name="h_pool", bufs=N_ROUNDS))
+        grouped = stack.enter_context(tc.tile_pool(name="grouped", bufs=3))
+        packed = stack.enter_context(tc.tile_pool(name="packed", bufs=6))
+        soft = stack.enter_context(tc.tile_pool(name="soft", bufs=2))
+        tp_psum = stack.enter_context(tc.psum_pool(name="tp_psum", bufs=2))
+        acc_psum = stack.enter_context(tc.psum_pool(name="acc_psum", bufs=3))
+        sc_psum = stack.enter_context(tc.psum_pool(name="sc_psum", bufs=1))
+
+        a_planes = const.tile([P, PASSES, D], U8, align_bytes=64)
+        nc.vector.memset(a_planes[:].rearrange("p g n -> p (g n)").bitcast(I32), 0)
+        warm = const.tile([P, 1], F32)
+        nc.vector.memset(warm[:], 0.0)
+        nc.scalar.activation(out=warm[:], in_=warm[:], func=EXP)
+        ident_f32 = const.tile([P, P], F32)
+        make_identity(nc, ident_f32[:])
+        ident_bf16 = const.tile([P, P], BF16)
+        make_identity(nc, ident_bf16[:])
+        mask = const.tile([P, P], F32)
+        nc.gpsimd.memset(mask[:], 0.0)
+        nc.gpsimd.affine_select(
+            out=mask[:], in_=mask[:], compare_op=ALU.is_ge, fill=NEG_INF,
+            base=0, pattern=[[-1, P]], channel_multiplier=1,
+        )
+
+        h_rounds = h.flatten_outer_dims().rearrange("(r c p) f -> r p c f", c=ROUND, p=P)
+        a_words = const.tile([P, PASSES, PACK * D], U8, align_bytes=64)
+        scale_rows = A_scales.bitcast(I32)
+        h_tiles = []
+        for r in range(N_ROUNDS):
+            h_sb = h_pool.tile([P, ROUND, D], BF16)
+            nc.sync.dma_start(out=h_sb[:], in_=h_rounds[r])
+            h_tiles.append(h_sb)
+            if r == 0:
+                for row in range(4):
+                    nc.sync.dma_start(
+                        out=a_planes[row:P:32, :, :].bitcast(I32),
+                        in_=scale_rows[:, row:16:4, :].rearrange("g q n -> q g n"),
+                    )
+                for gd in range(PASSES):
+                    nc.sync.dma_start(
+                        out=a_words[:, gd, :].bitcast(I32),
+                        in_=A_words[gd].rearrange("p n t -> p (n t)").bitcast(I32),
+                    )
+
+        out_view = out.rearrange("(c q) o t s -> (q o t) c s", q=SEQS_IN_CHUNK)
+
+        def quantise(values, name):
+            words = packed.tile([P, ROUND, PASSES, CHUNK], U32, align_bytes=64, name=name + "_words")
+            scales = packed.tile([P, ROUND, PASSES, CHUNK], U8, align_bytes=64, name=name + "_scales")
+            nc.vector.quantize_mx(
+                out=words[:].rearrange("p c g k -> p (c g k)").bitcast(FP8X4),
+                scales=scales[:].rearrange("p c g k -> p (c g k)"),
+                in_=values[:].rearrange("p c g k t -> p (c g k t)"),
+            )
+            return words, scales
+
+        first_layout = {}
+        second_layout = {}
+        product = {}
+
+        def transpose_round(r):
+            h_sb = h_tiles[r]
+            g1 = grouped.tile([P, ROUND, PASSES, CHUNK, PACK], BF16, align_bytes=64)
+            g2 = grouped.tile([P, ROUND, PASSES, CHUNK, PACK], BF16, align_bytes=64)
+            for c in range(ROUND):
+                pairs = h_sb[:, c, :].bitcast(F32)
+                tp1 = tp_psum.tile([P, PASSES, 2, CHUNK], F32)
+                for g in range(PASSES):
+                    for u in range(2):
+                        nc.tensor.transpose(
+                            tp1[:, g, u, :], pairs[:, 256 * g + u : 256 * (g + 1) : 2], ident_f32[:]
+                        )
+                nc.scalar.copy(out=g1[:, c].bitcast(F32), in_=tp1[:].rearrange("p g u k -> p g k u"))
+            for c in range(ROUND):
+                tp2 = tp_psum.tile([P, PASSES * PACK, CHUNK], BF16)
+                for m in range(PASSES * PACK):
+                    nc.tensor.transpose(tp2[:, m, :], h_sb[:, c, P * m : P * (m + 1)], ident_bf16[:])
+                by_token = tp2[:].rearrange("p (g t) k -> p g k t", t=PACK)
+                if (ROUND * r + c) % SCALAR_TAKES_EVERY == 0:
+                    nc.scalar.copy(out=g2[:, c], in_=by_token)
+                else:
+                    nc.vector.tensor_copy(out=g2[:, c], in_=by_token)
+            first_layout[r] = quantise(g1, "h1")
+            second_layout[r] = quantise(g2, "h2")
+
+        def first_product(r):
+            h1_words, h1_scales = first_layout[r]
+            ga = grouped.tile([P, ROUND, PASSES, CHUNK, PACK], BF16, align_bytes=64)
+            for c in range(ROUND):
+                for ge in range(PASSES):
+                    acc = acc_psum.tile([P, PACK, CHUNK], F32)
+                    for t in range(PACK):
+                        m = PACK * ge + t
+                        for gd in range(PASSES):
+                            nc.tensor.matmul_mx(
+                                out=acc[:, t, :],
+                                lhsT=a_words[:, gd, PACK * P * m : PACK * P * (m + 1)].bitcast(FP8X4),
+                                lhsT_scale=a_planes[:, gd, P * m : P * (m + 1)],
+                                rhs=h1_words[:, c, gd, :].bitcast(FP8X4),
+                                rhs_scale=h1_scales[:, c, gd, :],
+                                start=(gd == 0),
+                                stop=(gd == PASSES - 1),
+                            )
+                    nc.scalar.copy(out=ga[:, c, ge], in_=acc[:].rearrange("p t k -> p k t"))
+            product[r] = quantise(ga, "ha")
+
+        def second_product_and_softmax(quad):
+            scores = sc_psum.tile([P, QUAD, CHUNK], F32)
+            for i in range(QUAD):
+                r, c = divmod(QUAD * quad + i, ROUND)
+                ha_words, ha_scales = product[r]
+                h2_words, h2_scales = second_layout[r]
+                for ge in range(PASSES):
+                    nc.tensor.matmul_mx(
+                        out=scores[:, i, :],
+                        lhsT=ha_words[:, c, ge, :].bitcast(FP8X4),
+                        lhsT_scale=ha_scales[:, c, ge, :],
+                        rhs=h2_words[:, c, ge, :].bitcast(FP8X4),
+                        rhs_scale=h2_scales[:, c, ge, :],
+                        start=(ge == 0),
+                        stop=(ge == PASSES - 1),
+                    )
+            masked = soft.tile([P, QUAD, T], F32)
+            for q in range(SEQS_IN_CHUNK):
+                own = slice(T * q, T * (q + 1))
+                nc.vector.tensor_tensor(
+                    out=masked[own, :, :],
+                    in0=scores[own, :, own],
+                    in1=mask[own, own].unsqueeze(1).to_broadcast([T, QUAD, T]),
+                    op=ALU.add,
+                )
+            top = soft.tile([P, QUAD], F32)
+            nc.vector.tensor_reduce(out=top[:], in_=masked[:], axis=LAST_AXIS, op=ALU.max)
+            shifted = soft.tile([P, QUAD, T], F32)
+            nc.vector.tensor_tensor(
+                out=shifted[:], in0=masked[:], in1=top[:].unsqueeze(2).to_broadcast([P, QUAD, T]),
+                op=ALU.subtract,
+            )
+            expd = soft.tile([P, QUAD, T], F32)
+            nc.scalar.activation(out=expd[:], in_=shifted[:], func=EXP)
+            total = soft.tile([P, QUAD], F32)
+            nc.vector.tensor_reduce(out=total[:], in_=expd[:], axis=LAST_AXIS, op=ALU.add)
+            inverse = soft.tile([P, QUAD], F32)
+            nc.vector.reciprocal(out=inverse[:], in_=total[:])
+            attn = soft.tile([P, QUAD, T], F32)
+            nc.vector.tensor_tensor(
+                out=attn[:], in0=expd[:], in1=inverse[:].unsqueeze(2).to_broadcast([P, QUAD, T]),
+                op=ALU.mult,
+            )
+            nc.sync.dma_start(out=out_view[:, QUAD * quad : QUAD * (quad + 1), :], in_=attn[:])
+
+        for step in range(N_ROUNDS + 2):
+            if step < N_ROUNDS:
+                transpose_round(step)
+            if 1 <= step <= N_ROUNDS:
+                first_product(step - 1)
+            if step >= 2 and (step - 2) % ROUNDS_IN_QUAD == ROUNDS_IN_QUAD - 1:
+                second_product_and_softmax((step - 2) // ROUNDS_IN_QUAD)

@@ -19,13 +19,16 @@ K_PASS = P * PACK
 SEQS, T, D = 128, 32, 1024
 PASSES = D // K_PASS
 CHUNK = P
+N_CHUNKS = SEQS * T // CHUNK
 SEQS_IN_CHUNK = CHUNK // T
-ROUND = 2
-N_ROUNDS = SEQS * T // (CHUNK * ROUND)
-QUAD = 4
-ROUNDS_IN_QUAD = QUAD // ROUND
+ROUND = 4
+N_ROUNDS = N_CHUNKS // ROUND
+LOAD = 2
+SEGMENTS = D // P
+BLOCK = P // SEGMENTS
+BLOCKS = CHUNK // BLOCK
 NEG_INF = -1e30
-SCALAR_TAKES_EVERY = 4
+SECOND_AFTER = 1
 
 FLOPS = 2 * SEQS * (T - 1) * D * D + 2 * SEQS * (T - 1) * T * D
 
@@ -33,14 +36,15 @@ FLOPS = 2 * SEQS * (T - 1) * D * D + 2 * SEQS * (T - 1) * T * D
 def tile_causalselfattention_pa_t_e_kernel(tc, h, A_words, A_scales, out):
     nc = tc.nc
     with ExitStack() as stack:
+        stack.enter_context(tc.manual_schedule())
         const = stack.enter_context(tc.tile_pool(name="const", bufs=1))
-        h_pool = stack.enter_context(tc.tile_pool(name="h_pool", bufs=N_ROUNDS))
+        h_pool = stack.enter_context(tc.tile_pool(name="h_pool", bufs=N_CHUNKS // LOAD))
         grouped = stack.enter_context(tc.tile_pool(name="grouped", bufs=3))
-        packed = stack.enter_context(tc.tile_pool(name="packed", bufs=6))
+        packed = stack.enter_context(tc.tile_pool(name="packed", bufs=2 * ROUND))
         soft = stack.enter_context(tc.tile_pool(name="soft", bufs=2))
-        tp_psum = stack.enter_context(tc.psum_pool(name="tp_psum", bufs=2))
-        acc_psum = stack.enter_context(tc.psum_pool(name="acc_psum", bufs=3))
-        sc_psum = stack.enter_context(tc.psum_pool(name="sc_psum", bufs=1))
+        results = stack.enter_context(tc.tile_pool(name="results", bufs=N_ROUNDS))
+        tp_psum = stack.enter_context(tc.psum_pool(name="tp_psum", bufs=4))
+        mx_psum = stack.enter_context(tc.psum_pool(name="mx_psum", bufs=4))
 
         a_planes = const.tile([P, PASSES, D], U8, align_bytes=64)
         nc.vector.memset(a_planes[:].rearrange("p g n -> p (g n)").bitcast(I32), 0)
@@ -58,15 +62,28 @@ def tile_causalselfattention_pa_t_e_kernel(tc, h, A_words, A_scales, out):
             base=0, pattern=[[-1, P]], channel_multiplier=1,
         )
 
-        h_rounds = h.flatten_outer_dims().rearrange("(r c p) f -> r p c f", c=ROUND, p=P)
+        tokens = h.flatten_outer_dims()
+        by_token = tokens.rearrange("(l c p) f -> l p c f", c=LOAD, p=P)
+        by_segment = tokens.rearrange("n (s f) -> (n s) f", f=P).rearrange(
+            "(l b p) f -> l p b f", b=LOAD * BLOCKS, p=P
+        )
         a_words = const.tile([P, PASSES, PACK * D], U8, align_bytes=64)
         scale_rows = A_scales.bitcast(I32)
-        h_tiles = []
-        for r in range(N_ROUNDS):
-            h_sb = h_pool.tile([P, ROUND, D], BF16)
-            nc.sync.dma_start(out=h_sb[:], in_=h_rounds[r])
-            h_tiles.append(h_sb)
-            if r == 0:
+        token_tiles = []
+        segment_tiles = []
+        loads_in_round = ROUND // LOAD
+        for r in range(N_ROUNDS + 2):
+            for l in range(loads_in_round * (r - 2), loads_in_round * (r - 1)):
+                if l >= 0:
+                    h_segments = h_pool.tile([P, LOAD * BLOCKS, P], BF16)
+                    nc.sync.dma_start(out=h_segments[:], in_=by_segment[l])
+                    segment_tiles.append(h_segments)
+            for l in range(loads_in_round * r, loads_in_round * (r + 1)):
+                if l < N_CHUNKS // LOAD:
+                    h_tokens = h_pool.tile([P, LOAD, D], BF16)
+                    nc.sync.dma_start(out=h_tokens[:], in_=by_token[l])
+                    token_tiles.append(h_tokens)
+            if r == 1:
                 for row in range(4):
                     nc.sync.dma_start(
                         out=a_planes[row:P:32, :, :].bitcast(I32),
@@ -80,115 +97,155 @@ def tile_causalselfattention_pa_t_e_kernel(tc, h, A_words, A_scales, out):
 
         out_view = out.rearrange("(c q) o t s -> (q o t) c s", q=SEQS_IN_CHUNK)
 
-        def quantise(values, name):
-            words = packed.tile([P, ROUND, PASSES, CHUNK], U32, align_bytes=64, name=name + "_words")
-            scales = packed.tile([P, ROUND, PASSES, CHUNK], U8, align_bytes=64, name=name + "_scales")
+        values = {}
+        codes = {}
+
+        def new_values(kind, j):
+            tile = grouped.tile([P, PASSES, CHUNK, PACK], BF16, align_bytes=64, name=kind + "_values")
+            values[(kind, j)] = tile
+            return tile
+
+        def pack(kind, j):
+            words = packed.tile([P, PASSES, CHUNK], U32, align_bytes=64, name=kind + "_words")
+            scales = packed.tile([P, PASSES, CHUNK], U8, align_bytes=64, name=kind + "_scales")
             nc.vector.quantize_mx(
-                out=words[:].rearrange("p c g k -> p (c g k)").bitcast(FP8X4),
-                scales=scales[:].rearrange("p c g k -> p (c g k)"),
-                in_=values[:].rearrange("p c g k t -> p (c g k t)"),
+                out=words[:].rearrange("p g k -> p (g k)").bitcast(FP8X4),
+                scales=scales[:].rearrange("p g k -> p (g k)"),
+                in_=values[(kind, j)][:].rearrange("p g k t -> p (g k t)"),
             )
-            return words, scales
+            codes[(kind, j)] = (words, scales)
 
-        first_layout = {}
-        second_layout = {}
-        product = {}
+        def transpose_first(j):
+            pairs = token_tiles[j // LOAD][:, j % LOAD, :].bitcast(F32)
+            tp1 = tp_psum.tile([P, PASSES, 2, CHUNK], F32, tag="tp")
+            for g in range(PASSES):
+                for u in range(2):
+                    nc.tensor.transpose(
+                        tp1[:, g, u, :], pairs[:, 256 * g + u : 256 * (g + 1) : 2], ident_f32[:]
+                    )
+            nc.scalar.copy(
+                out=new_values("h1", j)[:].bitcast(F32), in_=tp1[:].rearrange("p g u k -> p g k u")
+            )
 
-        def transpose_round(r):
-            h_sb = h_tiles[r]
-            g1 = grouped.tile([P, ROUND, PASSES, CHUNK, PACK], BF16, align_bytes=64)
-            g2 = grouped.tile([P, ROUND, PASSES, CHUNK, PACK], BF16, align_bytes=64)
-            for c in range(ROUND):
-                pairs = h_sb[:, c, :].bitcast(F32)
-                tp1 = tp_psum.tile([P, PASSES, 2, CHUNK], F32)
-                for g in range(PASSES):
-                    for u in range(2):
-                        nc.tensor.transpose(
-                            tp1[:, g, u, :], pairs[:, 256 * g + u : 256 * (g + 1) : 2], ident_f32[:]
+        def transpose_second(j):
+            h_segments = segment_tiles[j // LOAD]
+            tp2 = tp_psum.tile([P, BLOCKS, P], BF16, tag="tp")
+            for b in range(BLOCKS):
+                nc.tensor.transpose(tp2[:, b, :], h_segments[:, BLOCKS * (j % LOAD) + b, :], ident_bf16[:])
+            by_pass = tp2[:].bitcast(F32).rearrange("p b (k g w) -> p g (b k) w", k=BLOCK, g=PASSES)
+            if j % 2 == 0:
+                nc.scalar.copy(out=new_values("h2", j)[:].bitcast(F32), in_=by_pass)
+            else:
+                nc.vector.tensor_copy(out=new_values("h2", j)[:].bitcast(F32), in_=by_pass)
+
+        def first_product(j):
+            h1_words, h1_scales = codes[("h1", j)]
+            ha_values = new_values("ha", j)
+            for ge in range(PASSES):
+                acc = mx_psum.tile([P, PACK, CHUNK], F32, tag="mx")
+                for t in range(PACK):
+                    m = PACK * ge + t
+                    for gd in range(PASSES):
+                        nc.tensor.matmul_mx(
+                            out=acc[:, t, :],
+                            lhsT=a_words[:, gd, PACK * P * m : PACK * P * (m + 1)].bitcast(FP8X4),
+                            lhsT_scale=a_planes[:, gd, P * m : P * (m + 1)],
+                            rhs=h1_words[:, gd, :].bitcast(FP8X4),
+                            rhs_scale=h1_scales[:, gd, :],
+                            start=(gd == 0),
+                            stop=(gd == PASSES - 1),
                         )
-                nc.scalar.copy(out=g1[:, c].bitcast(F32), in_=tp1[:].rearrange("p g u k -> p g k u"))
-            for c in range(ROUND):
-                tp2 = tp_psum.tile([P, PASSES * PACK, CHUNK], BF16)
-                for m in range(PASSES * PACK):
-                    nc.tensor.transpose(tp2[:, m, :], h_sb[:, c, P * m : P * (m + 1)], ident_bf16[:])
-                by_token = tp2[:].rearrange("p (g t) k -> p g k t", t=PACK)
-                if (ROUND * r + c) % SCALAR_TAKES_EVERY == 0:
-                    nc.scalar.copy(out=g2[:, c], in_=by_token)
+                if j % 2 == 1 and ge == PASSES - 1:
+                    nc.vector.tensor_copy(out=ha_values[:, ge], in_=acc[:].rearrange("p t k -> p k t"))
                 else:
-                    nc.vector.tensor_copy(out=g2[:, c], in_=by_token)
-            first_layout[r] = quantise(g1, "h1")
-            second_layout[r] = quantise(g2, "h2")
+                    nc.scalar.copy(out=ha_values[:, ge], in_=acc[:].rearrange("p t k -> p k t"))
 
-        def first_product(r):
-            h1_words, h1_scales = first_layout[r]
-            ga = grouped.tile([P, ROUND, PASSES, CHUNK, PACK], BF16, align_bytes=64)
+        softmax_tiles = {}
+
+        def second_product(r):
+            scores = mx_psum.tile([P, ROUND, CHUNK], F32, tag="mx")
             for c in range(ROUND):
-                for ge in range(PASSES):
-                    acc = acc_psum.tile([P, PACK, CHUNK], F32)
-                    for t in range(PACK):
-                        m = PACK * ge + t
-                        for gd in range(PASSES):
-                            nc.tensor.matmul_mx(
-                                out=acc[:, t, :],
-                                lhsT=a_words[:, gd, PACK * P * m : PACK * P * (m + 1)].bitcast(FP8X4),
-                                lhsT_scale=a_planes[:, gd, P * m : P * (m + 1)],
-                                rhs=h1_words[:, c, gd, :].bitcast(FP8X4),
-                                rhs_scale=h1_scales[:, c, gd, :],
-                                start=(gd == 0),
-                                stop=(gd == PASSES - 1),
-                            )
-                    nc.scalar.copy(out=ga[:, c, ge], in_=acc[:].rearrange("p t k -> p k t"))
-            product[r] = quantise(ga, "ha")
-
-        def second_product_and_softmax(quad):
-            scores = sc_psum.tile([P, QUAD, CHUNK], F32)
-            for i in range(QUAD):
-                r, c = divmod(QUAD * quad + i, ROUND)
-                ha_words, ha_scales = product[r]
-                h2_words, h2_scales = second_layout[r]
+                ha_words, ha_scales = codes[("ha", ROUND * r + c)]
+                h2_words, h2_scales = codes[("h2", ROUND * r + c)]
                 for ge in range(PASSES):
                     nc.tensor.matmul_mx(
-                        out=scores[:, i, :],
-                        lhsT=ha_words[:, c, ge, :].bitcast(FP8X4),
-                        lhsT_scale=ha_scales[:, c, ge, :],
-                        rhs=h2_words[:, c, ge, :].bitcast(FP8X4),
-                        rhs_scale=h2_scales[:, c, ge, :],
+                        out=scores[:, c, :],
+                        lhsT=ha_words[:, ge, :].bitcast(FP8X4),
+                        lhsT_scale=ha_scales[:, ge, :],
+                        rhs=h2_words[:, ge, :].bitcast(FP8X4),
+                        rhs_scale=h2_scales[:, ge, :],
                         start=(ge == 0),
                         stop=(ge == PASSES - 1),
                     )
-            masked = soft.tile([P, QUAD, T], F32)
+            softmax_tiles[("scores", r)] = scores
+
+        def mask_and_shift(r):
+            scores = softmax_tiles[("scores", r)]
+            masked = soft.tile([P, ROUND, T], F32)
             for q in range(SEQS_IN_CHUNK):
                 own = slice(T * q, T * (q + 1))
                 nc.vector.tensor_tensor(
                     out=masked[own, :, :],
                     in0=scores[own, :, own],
-                    in1=mask[own, own].unsqueeze(1).to_broadcast([T, QUAD, T]),
+                    in1=mask[own, own].unsqueeze(1).to_broadcast([T, ROUND, T]),
                     op=ALU.add,
                 )
-            top = soft.tile([P, QUAD], F32)
+            top = soft.tile([P, ROUND], F32)
             nc.vector.tensor_reduce(out=top[:], in_=masked[:], axis=LAST_AXIS, op=ALU.max)
-            shifted = soft.tile([P, QUAD, T], F32)
+            shifted = soft.tile([P, ROUND, T], F32)
             nc.vector.tensor_tensor(
-                out=shifted[:], in0=masked[:], in1=top[:].unsqueeze(2).to_broadcast([P, QUAD, T]),
+                out=shifted[:], in0=masked[:], in1=top[:].unsqueeze(2).to_broadcast([P, ROUND, T]),
                 op=ALU.subtract,
             )
-            expd = soft.tile([P, QUAD, T], F32)
-            nc.scalar.activation(out=expd[:], in_=shifted[:], func=EXP)
-            total = soft.tile([P, QUAD], F32)
+            softmax_tiles[("shifted", r)] = shifted
+
+        def exponentials(r):
+            expd = soft.tile([P, ROUND, T], F32)
+            nc.scalar.activation(out=expd[:], in_=softmax_tiles[("shifted", r)][:], func=EXP)
+            softmax_tiles[("expd", r)] = expd
+
+        def normalise_and_store(r):
+            expd = softmax_tiles[("expd", r)]
+            total = soft.tile([P, ROUND], F32)
             nc.vector.tensor_reduce(out=total[:], in_=expd[:], axis=LAST_AXIS, op=ALU.add)
-            inverse = soft.tile([P, QUAD], F32)
+            inverse = soft.tile([P, ROUND], F32)
             nc.vector.reciprocal(out=inverse[:], in_=total[:])
-            attn = soft.tile([P, QUAD, T], F32)
+            attn = results.tile([P, ROUND, T], F32)
             nc.vector.tensor_tensor(
-                out=attn[:], in0=expd[:], in1=inverse[:].unsqueeze(2).to_broadcast([P, QUAD, T]),
+                out=attn[:], in0=expd[:], in1=inverse[:].unsqueeze(2).to_broadcast([P, ROUND, T]),
                 op=ALU.mult,
             )
-            nc.sync.dma_start(out=out_view[:, QUAD * quad : QUAD * (quad + 1), :], in_=attn[:])
+            nc.sync.dma_start(out=out_view[:, ROUND * r : ROUND * (r + 1), :], in_=attn[:])
 
+        seconds_done = 0
         for step in range(N_ROUNDS + 2):
-            if step < N_ROUNDS:
-                transpose_round(step)
-            if 1 <= step <= N_ROUNDS:
-                first_product(step - 1)
-            if step >= 2 and (step - 2) % ROUNDS_IN_QUAD == ROUNDS_IN_QUAD - 1:
-                second_product_and_softmax((step - 2) // ROUNDS_IN_QUAD)
+            firsts = list(range(ROUND * step, ROUND * (step + 1))) if step < N_ROUNDS else []
+            seconds_due = ROUND * (step - 1) if step < N_ROUNDS else N_CHUNKS
+            seconds = list(range(seconds_done, max(seconds_done, seconds_due)))
+            seconds_done += len(seconds)
+            for turn in range(max(len(firsts), len(seconds)) + 1):
+                if turn < len(firsts):
+                    transpose_first(firsts[turn])
+                if turn < len(seconds):
+                    transpose_second(seconds[turn])
+                if 1 <= turn <= len(firsts):
+                    pack("h1", firsts[turn - 1])
+                if 1 <= turn <= len(seconds):
+                    pack("h2", seconds[turn - 1])
+            first_active = 1 <= step <= N_ROUNDS
+            second_active = 0 <= step - 2 < N_ROUNDS
+            for c in range(ROUND):
+                j = ROUND * (step - 1) + c
+                if first_active:
+                    first_product(j)
+                    if c > 0:
+                        pack("ha", j - 1)
+                if second_active and c == SECOND_AFTER:
+                    second_product(step - 2)
+                    mask_and_shift(step - 2)
+                if second_active and c == SECOND_AFTER + 1:
+                    exponentials(step - 2)
+            if first_active:
+                pack("ha", ROUND * step - 1)
+            if second_active:
+                normalise_and_store(step - 2)

@@ -21,14 +21,11 @@ PASSES = D // K_PASS
 CHUNK = P
 N_CHUNKS = SEQS * T // CHUNK
 SEQS_IN_CHUNK = CHUNK // T
-ROUND = 4
+ROUND = 2
 N_ROUNDS = N_CHUNKS // ROUND
-LOAD = 2
-SEGMENTS = D // P
-BLOCK = P // SEGMENTS
-BLOCKS = CHUNK // BLOCK
+QUAD = 4
+ROUNDS_IN_QUAD = QUAD // ROUND
 NEG_INF = -1e30
-SECOND_AFTER = 1
 
 FLOPS = 2 * SEQS * (T - 1) * D * D + 2 * SEQS * (T - 1) * T * D
 
@@ -38,11 +35,11 @@ def tile_causalselfattention_pa_t_e_kernel(tc, h, A_words, A_scales, out):
     with ExitStack() as stack:
         stack.enter_context(tc.manual_schedule())
         const = stack.enter_context(tc.tile_pool(name="const", bufs=1))
-        h_pool = stack.enter_context(tc.tile_pool(name="h_pool", bufs=N_CHUNKS // LOAD))
+        h_pool = stack.enter_context(tc.tile_pool(name="h_pool", bufs=N_ROUNDS))
         grouped = stack.enter_context(tc.tile_pool(name="grouped", bufs=3))
-        packed = stack.enter_context(tc.tile_pool(name="packed", bufs=2 * ROUND))
+        packed = stack.enter_context(tc.tile_pool(name="packed", bufs=2 * QUAD))
         soft = stack.enter_context(tc.tile_pool(name="soft", bufs=2))
-        results = stack.enter_context(tc.tile_pool(name="results", bufs=N_ROUNDS))
+        results = stack.enter_context(tc.tile_pool(name="results", bufs=N_CHUNKS // QUAD))
         tp_psum = stack.enter_context(tc.psum_pool(name="tp_psum", bufs=4))
         mx_psum = stack.enter_context(tc.psum_pool(name="mx_psum", bufs=4))
 
@@ -62,27 +59,14 @@ def tile_causalselfattention_pa_t_e_kernel(tc, h, A_words, A_scales, out):
             base=0, pattern=[[-1, P]], channel_multiplier=1,
         )
 
-        tokens = h.flatten_outer_dims()
-        by_token = tokens.rearrange("(l c p) f -> l p c f", c=LOAD, p=P)
-        by_segment = tokens.rearrange("n (s f) -> (n s) f", f=P).rearrange(
-            "(l b p) f -> l p b f", b=LOAD * BLOCKS, p=P
-        )
+        h_rounds = h.flatten_outer_dims().rearrange("(r c p) f -> r p c f", c=ROUND, p=P)
         a_words = const.tile([P, PASSES, PACK * D], U8, align_bytes=64)
         scale_rows = A_scales.bitcast(I32)
-        token_tiles = []
-        segment_tiles = []
-        loads_in_round = ROUND // LOAD
-        for r in range(N_ROUNDS + 2):
-            for l in range(loads_in_round * (r - 2), loads_in_round * (r - 1)):
-                if l >= 0:
-                    h_segments = h_pool.tile([P, LOAD * BLOCKS, P], BF16)
-                    nc.sync.dma_start(out=h_segments[:], in_=by_segment[l])
-                    segment_tiles.append(h_segments)
-            for l in range(loads_in_round * r, loads_in_round * (r + 1)):
-                if l < N_CHUNKS // LOAD:
-                    h_tokens = h_pool.tile([P, LOAD, D], BF16)
-                    nc.sync.dma_start(out=h_tokens[:], in_=by_token[l])
-                    token_tiles.append(h_tokens)
+        h_tiles = []
+        for r in range(N_ROUNDS):
+            h_sb = h_pool.tile([P, ROUND, D], BF16)
+            nc.sync.dma_start(out=h_sb[:], in_=h_rounds[r])
+            h_tiles.append(h_sb)
             if r == 1:
                 for row in range(4):
                     nc.sync.dma_start(
@@ -101,9 +85,9 @@ def tile_causalselfattention_pa_t_e_kernel(tc, h, A_words, A_scales, out):
         codes = {}
 
         def new_values(kind, j):
-            tile = grouped.tile([P, PASSES, CHUNK, PACK], BF16, align_bytes=64, name=kind + "_values")
-            values[(kind, j)] = tile
-            return tile
+            fresh = grouped.tile([P, PASSES, CHUNK, PACK], BF16, align_bytes=64, name=kind + "_values")
+            values[(kind, j)] = fresh
+            return fresh
 
         def pack(kind, j):
             words = packed.tile([P, PASSES, CHUNK], U32, align_bytes=64, name=kind + "_words")
@@ -116,7 +100,7 @@ def tile_causalselfattention_pa_t_e_kernel(tc, h, A_words, A_scales, out):
             codes[(kind, j)] = (words, scales)
 
         def transpose_first(j):
-            pairs = token_tiles[j // LOAD][:, j % LOAD, :].bitcast(F32)
+            pairs = h_tiles[j // ROUND][:, j % ROUND, :].bitcast(F32)
             tp1 = tp_psum.tile([P, PASSES, 2, CHUNK], F32, tag="tp")
             for g in range(PASSES):
                 for u in range(2):
@@ -128,15 +112,15 @@ def tile_causalselfattention_pa_t_e_kernel(tc, h, A_words, A_scales, out):
             )
 
         def transpose_second(j):
-            h_segments = segment_tiles[j // LOAD]
-            tp2 = tp_psum.tile([P, BLOCKS, P], BF16, tag="tp")
-            for b in range(BLOCKS):
-                nc.tensor.transpose(tp2[:, b, :], h_segments[:, BLOCKS * (j % LOAD) + b, :], ident_bf16[:])
-            by_pass = tp2[:].bitcast(F32).rearrange("p b (k g w) -> p g (b k) w", k=BLOCK, g=PASSES)
+            h_sb = h_tiles[j // ROUND]
+            tp2 = tp_psum.tile([P, PASSES * PACK, CHUNK], BF16, tag="tp")
+            for m in range(PASSES * PACK):
+                nc.tensor.transpose(tp2[:, m, :], h_sb[:, j % ROUND, P * m : P * (m + 1)], ident_bf16[:])
+            by_token = tp2[:].rearrange("p (g t) k -> p g k t", t=PACK)
             if j % 2 == 0:
-                nc.scalar.copy(out=new_values("h2", j)[:].bitcast(F32), in_=by_pass)
+                nc.scalar.copy(out=new_values("h2", j)[:], in_=by_token)
             else:
-                nc.vector.tensor_copy(out=new_values("h2", j)[:].bitcast(F32), in_=by_pass)
+                nc.vector.tensor_copy(out=new_values("h2", j)[:], in_=by_token)
 
         def first_product(j):
             h1_words, h1_scales = codes[("h1", j)]
@@ -162,11 +146,11 @@ def tile_causalselfattention_pa_t_e_kernel(tc, h, A_words, A_scales, out):
 
         softmax_tiles = {}
 
-        def second_product(r):
-            scores = mx_psum.tile([P, ROUND, CHUNK], F32, tag="mx")
-            for c in range(ROUND):
-                ha_words, ha_scales = codes[("ha", ROUND * r + c)]
-                h2_words, h2_scales = codes[("h2", ROUND * r + c)]
+        def second_product(quad):
+            scores = mx_psum.tile([P, QUAD, CHUNK], F32, tag="mx")
+            for c in range(QUAD):
+                ha_words, ha_scales = codes[("ha", QUAD * quad + c)]
+                h2_words, h2_scales = codes[("h2", QUAD * quad + c)]
                 for ge in range(PASSES):
                     nc.tensor.matmul_mx(
                         out=scores[:, c, :],
@@ -177,75 +161,71 @@ def tile_causalselfattention_pa_t_e_kernel(tc, h, A_words, A_scales, out):
                         start=(ge == 0),
                         stop=(ge == PASSES - 1),
                     )
-            softmax_tiles[("scores", r)] = scores
+            softmax_tiles[("scores", quad)] = scores
 
-        def mask_and_shift(r):
-            scores = softmax_tiles[("scores", r)]
-            masked = soft.tile([P, ROUND, T], F32)
+        def mask_and_shift(quad):
+            scores = softmax_tiles[("scores", quad)]
+            masked = soft.tile([P, QUAD, T], F32)
             for q in range(SEQS_IN_CHUNK):
                 own = slice(T * q, T * (q + 1))
                 nc.vector.tensor_tensor(
                     out=masked[own, :, :],
                     in0=scores[own, :, own],
-                    in1=mask[own, own].unsqueeze(1).to_broadcast([T, ROUND, T]),
+                    in1=mask[own, own].unsqueeze(1).to_broadcast([T, QUAD, T]),
                     op=ALU.add,
                 )
-            top = soft.tile([P, ROUND], F32)
+            top = soft.tile([P, QUAD], F32)
             nc.vector.tensor_reduce(out=top[:], in_=masked[:], axis=LAST_AXIS, op=ALU.max)
-            shifted = soft.tile([P, ROUND, T], F32)
+            shifted = soft.tile([P, QUAD, T], F32)
             nc.vector.tensor_tensor(
-                out=shifted[:], in0=masked[:], in1=top[:].unsqueeze(2).to_broadcast([P, ROUND, T]),
+                out=shifted[:], in0=masked[:], in1=top[:].unsqueeze(2).to_broadcast([P, QUAD, T]),
                 op=ALU.subtract,
             )
-            softmax_tiles[("shifted", r)] = shifted
+            softmax_tiles[("shifted", quad)] = shifted
 
-        def exponentials(r):
-            expd = soft.tile([P, ROUND, T], F32)
-            nc.scalar.activation(out=expd[:], in_=softmax_tiles[("shifted", r)][:], func=EXP)
-            softmax_tiles[("expd", r)] = expd
+        def exponentials(quad):
+            expd = soft.tile([P, QUAD, T], F32)
+            nc.scalar.activation(out=expd[:], in_=softmax_tiles[("shifted", quad)][:], func=EXP)
+            softmax_tiles[("expd", quad)] = expd
 
-        def normalise_and_store(r):
-            expd = softmax_tiles[("expd", r)]
-            total = soft.tile([P, ROUND], F32)
+        def normalise_and_store(quad):
+            expd = softmax_tiles[("expd", quad)]
+            total = soft.tile([P, QUAD], F32)
             nc.vector.tensor_reduce(out=total[:], in_=expd[:], axis=LAST_AXIS, op=ALU.add)
-            inverse = soft.tile([P, ROUND], F32)
+            inverse = soft.tile([P, QUAD], F32)
             nc.vector.reciprocal(out=inverse[:], in_=total[:])
-            attn = results.tile([P, ROUND, T], F32)
+            attn = results.tile([P, QUAD, T], F32)
             nc.vector.tensor_tensor(
-                out=attn[:], in0=expd[:], in1=inverse[:].unsqueeze(2).to_broadcast([P, ROUND, T]),
+                out=attn[:], in0=expd[:], in1=inverse[:].unsqueeze(2).to_broadcast([P, QUAD, T]),
                 op=ALU.mult,
             )
-            nc.sync.dma_start(out=out_view[:, ROUND * r : ROUND * (r + 1), :], in_=attn[:])
+            nc.sync.dma_start(out=out_view[:, QUAD * quad : QUAD * (quad + 1), :], in_=attn[:])
 
-        seconds_done = 0
         for step in range(N_ROUNDS + 2):
-            firsts = list(range(ROUND * step, ROUND * (step + 1))) if step < N_ROUNDS else []
-            seconds_due = ROUND * (step - 1) if step < N_ROUNDS else N_CHUNKS
-            seconds = list(range(seconds_done, max(seconds_done, seconds_due)))
-            seconds_done += len(seconds)
-            for turn in range(max(len(firsts), len(seconds)) + 1):
-                if turn < len(firsts):
-                    transpose_first(firsts[turn])
-                if turn < len(seconds):
-                    transpose_second(seconds[turn])
-                if 1 <= turn <= len(firsts):
-                    pack("h1", firsts[turn - 1])
-                if 1 <= turn <= len(seconds):
-                    pack("h2", seconds[turn - 1])
+            if step < N_ROUNDS:
+                previous = None
+                for kind, transposes in (("h1", transpose_first), ("h2", transpose_second)):
+                    for j in range(ROUND * step, ROUND * (step + 1)):
+                        transposes(j)
+                        if previous:
+                            pack(*previous)
+                        previous = (kind, j)
+                pack(*previous)
             first_active = 1 <= step <= N_ROUNDS
-            second_active = 0 <= step - 2 < N_ROUNDS
+            quad, rest = divmod(step - 1 - ROUNDS_IN_QUAD, ROUNDS_IN_QUAD)
+            second_active = quad >= 0 and rest == 0
             for c in range(ROUND):
                 j = ROUND * (step - 1) + c
                 if first_active:
                     first_product(j)
                     if c > 0:
                         pack("ha", j - 1)
-                if second_active and c == SECOND_AFTER:
-                    second_product(step - 2)
-                    mask_and_shift(step - 2)
-                if second_active and c == SECOND_AFTER + 1:
-                    exponentials(step - 2)
+                if second_active and c == 0:
+                    second_product(quad)
+                    mask_and_shift(quad)
+                if second_active and c == 1:
+                    exponentials(quad)
             if first_active:
                 pack("ha", ROUND * step - 1)
             if second_active:
-                normalise_and_store(step - 2)
+                normalise_and_store(quad)

@@ -43,15 +43,14 @@ def tile_causalselfattention_pa_t_e_kernel(tc, h, A_words, A_scales, out):
         tp_psum = stack.enter_context(tc.psum_pool(name="tp_psum", bufs=4))
         mx_psum = stack.enter_context(tc.psum_pool(name="mx_psum", bufs=4))
 
+        raw_planes = const.tile([P, PASSES, D], U8, align_bytes=64)
+        nc.vector.memset(raw_planes[:].rearrange("p g n -> p (g n)").bitcast(I32), 0)
         a_planes = const.tile([P, PASSES, D], U8, align_bytes=64)
-        nc.vector.memset(a_planes[:].rearrange("p g n -> p (g n)").bitcast(I32), 0)
         warm = const.tile([P, 1], F32)
         nc.vector.memset(warm[:], 0.0)
         nc.scalar.activation(out=warm[:], in_=warm[:], func=EXP)
         ident_f32 = const.tile([P, P], F32)
         make_identity(nc, ident_f32[:])
-        ident_bf16 = const.tile([P, P], BF16)
-        make_identity(nc, ident_bf16[:])
         mask = const.tile([P, P], F32)
         nc.gpsimd.memset(mask[:], 0.0)
         nc.gpsimd.affine_select(
@@ -60,6 +59,7 @@ def tile_causalselfattention_pa_t_e_kernel(tc, h, A_words, A_scales, out):
         )
 
         h_rounds = h.flatten_outer_dims().rearrange("(r c p) f -> r p c f", c=ROUND, p=P)
+        raw_words = const.tile([P, PASSES, PACK * D], U8, align_bytes=64)
         a_words = const.tile([P, PASSES, PACK * D], U8, align_bytes=64)
         scale_rows = A_scales.bitcast(I32)
         h_tiles = []
@@ -70,14 +70,27 @@ def tile_causalselfattention_pa_t_e_kernel(tc, h, A_words, A_scales, out):
             if r == 1:
                 for row in range(4):
                     nc.sync.dma_start(
-                        out=a_planes[row:P:32, :, :].bitcast(I32),
+                        out=raw_planes[row:P:32, :, :].bitcast(I32),
                         in_=scale_rows[:, row:16:4, :].rearrange("g q n -> q g n"),
                     )
                 for gd in range(PASSES):
                     nc.sync.dma_start(
-                        out=a_words[:, gd, :].bitcast(I32),
+                        out=raw_words[:, gd, :].bitcast(I32),
                         in_=A_words[gd].rearrange("p n t -> p (n t)").bitcast(I32),
                     )
+
+        def reorder_a():
+            for t in range(PACK):
+                nc.vector.tensor_copy(
+                    out=a_planes[:].rearrange("p g (e t m) -> p t g e m", e=PASSES, t=PACK)[:, t],
+                    in_=raw_planes[:].rearrange("p g (e m t) -> p t g e m", e=PASSES, t=PACK)[:, t],
+                )
+            for ge in range(PASSES):
+                half = slice(K_PASS * ge, K_PASS * (ge + 1))
+                nc.vector.tensor_copy(
+                    out=a_words[:].bitcast(I32)[:, :, half].rearrange("p g (t m) -> p g t m", t=PACK),
+                    in_=raw_words[:].bitcast(I32)[:, :, half].rearrange("p g (m t) -> p g t m", t=PACK),
+                )
 
         out_view = out.rearrange("(c q) o t s -> (q o t) c s", q=SEQS_IN_CHUNK)
 
@@ -111,17 +124,6 @@ def tile_causalselfattention_pa_t_e_kernel(tc, h, A_words, A_scales, out):
                 out=new_values("h1", j)[:].bitcast(F32), in_=tp1[:].rearrange("p g u k -> p g k u")
             )
 
-        def transpose_second(j):
-            h_sb = h_tiles[j // ROUND]
-            tp2 = tp_psum.tile([P, PASSES * PACK, CHUNK], BF16, tag="tp")
-            for m in range(PASSES * PACK):
-                nc.tensor.transpose(tp2[:, m, :], h_sb[:, j % ROUND, P * m : P * (m + 1)], ident_bf16[:])
-            by_token = tp2[:].rearrange("p (g t) k -> p g k t", t=PACK)
-            if j % 2 == 0:
-                nc.scalar.copy(out=new_values("h2", j)[:], in_=by_token)
-            else:
-                nc.vector.tensor_copy(out=new_values("h2", j)[:], in_=by_token)
-
         def first_product(j):
             h1_words, h1_scales = codes[("h1", j)]
             ha_values = new_values("ha", j)
@@ -150,7 +152,7 @@ def tile_causalselfattention_pa_t_e_kernel(tc, h, A_words, A_scales, out):
             scores = mx_psum.tile([P, QUAD, CHUNK], F32, tag="mx")
             for c in range(QUAD):
                 ha_words, ha_scales = codes[("ha", QUAD * quad + c)]
-                h2_words, h2_scales = codes[("h2", QUAD * quad + c)]
+                h2_words, h2_scales = codes[("h1", QUAD * quad + c)]
                 for ge in range(PASSES):
                     nc.tensor.matmul_mx(
                         out=scores[:, c, :],
@@ -204,13 +206,14 @@ def tile_causalselfattention_pa_t_e_kernel(tc, h, A_words, A_scales, out):
         for step in range(N_ROUNDS + 2):
             if step < N_ROUNDS:
                 previous = None
-                for kind, transposes in (("h1", transpose_first), ("h2", transpose_second)):
-                    for j in range(ROUND * step, ROUND * (step + 1)):
-                        transposes(j)
-                        if previous:
-                            pack(*previous)
-                        previous = (kind, j)
+                for j in range(ROUND * step, ROUND * (step + 1)):
+                    transpose_first(j)
+                    if previous:
+                        pack(*previous)
+                    previous = ("h1", j)
                 pack(*previous)
+            if step == 0:
+                reorder_a()
             first_active = 1 <= step <= N_ROUNDS
             quad, rest = divmod(step - 1 - ROUNDS_IN_QUAD, ROUNDS_IN_QUAD)
             second_active = quad >= 0 and rest == 0

@@ -21,11 +21,12 @@ PASSES = D // K_PASS
 CHUNK = P
 N_CHUNKS = SEQS * T // CHUNK
 SEQS_IN_CHUNK = CHUNK // T
-ROUND = 2
-N_ROUNDS = N_CHUNKS // ROUND
-QUAD = 4
-ROUNDS_IN_QUAD = QUAD // ROUND
+LOAD = 2
+RUNS = (2, 2) + (4,) * 7
+GROUPS = (4,) * 8
 NEG_INF = -1e30
+
+assert sum(RUNS) == N_CHUNKS and sum(GROUPS) == N_CHUNKS
 
 FLOPS = 2 * SEQS * (T - 1) * D * D + 2 * SEQS * (T - 1) * T * D
 
@@ -35,11 +36,11 @@ def tile_causalselfattention_pa_t_e_kernel(tc, h, A_words, A_scales, out):
     with ExitStack() as stack:
         stack.enter_context(tc.manual_schedule())
         const = stack.enter_context(tc.tile_pool(name="const", bufs=1))
-        h_pool = stack.enter_context(tc.tile_pool(name="h_pool", bufs=N_ROUNDS))
+        h_pool = stack.enter_context(tc.tile_pool(name="h_pool", bufs=N_CHUNKS // LOAD))
         grouped = stack.enter_context(tc.tile_pool(name="grouped", bufs=3))
-        packed = stack.enter_context(tc.tile_pool(name="packed", bufs=2 * QUAD))
+        packed = stack.enter_context(tc.tile_pool(name="packed", bufs=2 * max(RUNS) + 4))
         soft = stack.enter_context(tc.tile_pool(name="soft", bufs=2))
-        results = stack.enter_context(tc.tile_pool(name="results", bufs=N_CHUNKS // QUAD))
+        results = stack.enter_context(tc.tile_pool(name="results", bufs=len(GROUPS)))
         tp_psum = stack.enter_context(tc.psum_pool(name="tp_psum", bufs=4))
         mx_psum = stack.enter_context(tc.psum_pool(name="mx_psum", bufs=4))
 
@@ -58,14 +59,14 @@ def tile_causalselfattention_pa_t_e_kernel(tc, h, A_words, A_scales, out):
             base=0, pattern=[[-1, P]], channel_multiplier=1,
         )
 
-        h_rounds = h.flatten_outer_dims().rearrange("(r c p) f -> r p c f", c=ROUND, p=P)
+        h_loads = h.flatten_outer_dims().rearrange("(r c p) f -> r p c f", c=LOAD, p=P)
         raw_words = const.tile([P, PASSES, PACK * D], U8, align_bytes=64)
         a_words = const.tile([P, PASSES, PACK * D], U8, align_bytes=64)
         scale_rows = A_scales.bitcast(I32)
         h_tiles = []
-        for r in range(N_ROUNDS):
-            h_sb = h_pool.tile([P, ROUND, D], BF16)
-            nc.sync.dma_start(out=h_sb[:], in_=h_rounds[r])
+        for r in range(N_CHUNKS // LOAD):
+            h_sb = h_pool.tile([P, LOAD, D], BF16)
+            nc.sync.dma_start(out=h_sb[:], in_=h_loads[r])
             h_tiles.append(h_sb)
             if r == 1:
                 for row in range(4):
@@ -112,20 +113,29 @@ def tile_causalselfattention_pa_t_e_kernel(tc, h, A_words, A_scales, out):
             )
             codes[(kind, j)] = (words, scales)
 
-        def transpose_first(j):
-            pairs = h_tiles[j // ROUND][:, j % ROUND, :].bitcast(F32)
-            tp1 = tp_psum.tile([P, PASSES, 2, CHUNK], F32, tag="tp")
+        def transposes(j):
+            pairs = h_tiles[j // LOAD][:, j % LOAD, :].bitcast(F32)
+            tp = tp_psum.tile([P, PASSES, 2, CHUNK], F32, tag="tp")
             for g in range(PASSES):
                 for u in range(2):
                     nc.tensor.transpose(
-                        tp1[:, g, u, :], pairs[:, 256 * g + u : 256 * (g + 1) : 2], ident_f32[:]
+                        tp[:, g, u, :], pairs[:, 256 * g + u : 256 * (g + 1) : 2], ident_f32[:]
                     )
             nc.scalar.copy(
-                out=new_values("h1", j)[:].bitcast(F32), in_=tp1[:].rearrange("p g u k -> p g k u")
+                out=new_values("h", j)[:].bitcast(F32), in_=tp[:].rearrange("p g u k -> p g k u")
             )
 
+        def run_of_transposes(chunks):
+            previous = None
+            for j in chunks:
+                transposes(j)
+                if previous is not None:
+                    pack("h", previous)
+                previous = j
+            pack("h", previous)
+
         def first_product(j):
-            h1_words, h1_scales = codes[("h1", j)]
+            h_words, h_scales = codes[("h", j)]
             ha_values = new_values("ha", j)
             for ge in range(PASSES):
                 acc = mx_psum.tile([P, PACK, CHUNK], F32, tag="mx")
@@ -136,8 +146,8 @@ def tile_causalselfattention_pa_t_e_kernel(tc, h, A_words, A_scales, out):
                             out=acc[:, t, :],
                             lhsT=a_words[:, gd, PACK * P * m : PACK * P * (m + 1)].bitcast(FP8X4),
                             lhsT_scale=a_planes[:, gd, P * m : P * (m + 1)],
-                            rhs=h1_words[:, gd, :].bitcast(FP8X4),
-                            rhs_scale=h1_scales[:, gd, :],
+                            rhs=h_words[:, gd, :].bitcast(FP8X4),
+                            rhs_scale=h_scales[:, gd, :],
                             start=(gd == 0),
                             stop=(gd == PASSES - 1),
                         )
@@ -148,87 +158,89 @@ def tile_causalselfattention_pa_t_e_kernel(tc, h, A_words, A_scales, out):
 
         softmax_tiles = {}
 
-        def second_product(quad):
-            scores = mx_psum.tile([P, QUAD, CHUNK], F32, tag="mx")
-            for c in range(QUAD):
-                ha_words, ha_scales = codes[("ha", QUAD * quad + c)]
-                h2_words, h2_scales = codes[("h1", QUAD * quad + c)]
+        def second_product(first, count):
+            scores = mx_psum.tile([P, count, CHUNK], F32, tag="mx")
+            for c in range(count):
+                ha_words, ha_scales = codes[("ha", first + c)]
+                h_words, h_scales = codes[("h", first + c)]
                 for ge in range(PASSES):
                     nc.tensor.matmul_mx(
                         out=scores[:, c, :],
                         lhsT=ha_words[:, ge, :].bitcast(FP8X4),
                         lhsT_scale=ha_scales[:, ge, :],
-                        rhs=h2_words[:, ge, :].bitcast(FP8X4),
-                        rhs_scale=h2_scales[:, ge, :],
+                        rhs=h_words[:, ge, :].bitcast(FP8X4),
+                        rhs_scale=h_scales[:, ge, :],
                         start=(ge == 0),
                         stop=(ge == PASSES - 1),
                     )
-            softmax_tiles[("scores", quad)] = scores
+            softmax_tiles[("scores", first)] = scores
 
-        def mask_and_shift(quad):
-            scores = softmax_tiles[("scores", quad)]
-            masked = soft.tile([P, QUAD, T], F32)
+        def mask_and_shift(first, count):
+            scores = softmax_tiles[("scores", first)]
+            masked = soft.tile([P, count, T], F32, name="masked")
             for q in range(SEQS_IN_CHUNK):
                 own = slice(T * q, T * (q + 1))
                 nc.vector.tensor_tensor(
                     out=masked[own, :, :],
                     in0=scores[own, :, own],
-                    in1=mask[own, own].unsqueeze(1).to_broadcast([T, QUAD, T]),
+                    in1=mask[own, own].unsqueeze(1).to_broadcast([T, count, T]),
                     op=ALU.add,
                 )
-            top = soft.tile([P, QUAD], F32)
+            top = soft.tile([P, count], F32, name="top")
             nc.vector.tensor_reduce(out=top[:], in_=masked[:], axis=LAST_AXIS, op=ALU.max)
-            shifted = soft.tile([P, QUAD, T], F32)
+            shifted = soft.tile([P, count, T], F32, name="shifted")
             nc.vector.tensor_tensor(
-                out=shifted[:], in0=masked[:], in1=top[:].unsqueeze(2).to_broadcast([P, QUAD, T]),
+                out=shifted[:], in0=masked[:], in1=top[:].unsqueeze(2).to_broadcast([P, count, T]),
                 op=ALU.subtract,
             )
-            softmax_tiles[("shifted", quad)] = shifted
+            softmax_tiles[("shifted", first)] = shifted
 
-        def exponentials(quad):
-            expd = soft.tile([P, QUAD, T], F32)
-            nc.scalar.activation(out=expd[:], in_=softmax_tiles[("shifted", quad)][:], func=EXP)
-            softmax_tiles[("expd", quad)] = expd
+        def exponentials(first, count):
+            expd = soft.tile([P, count, T], F32, name="expd")
+            nc.scalar.activation(out=expd[:], in_=softmax_tiles[("shifted", first)][:], func=EXP)
+            softmax_tiles[("expd", first)] = expd
 
-        def normalise_and_store(quad):
-            expd = softmax_tiles[("expd", quad)]
-            total = soft.tile([P, QUAD], F32)
+        def normalise_and_store(first, count):
+            expd = softmax_tiles[("expd", first)]
+            total = soft.tile([P, count], F32, name="total")
             nc.vector.tensor_reduce(out=total[:], in_=expd[:], axis=LAST_AXIS, op=ALU.add)
-            inverse = soft.tile([P, QUAD], F32)
+            inverse = soft.tile([P, count], F32, name="inverse")
             nc.vector.reciprocal(out=inverse[:], in_=total[:])
-            attn = results.tile([P, QUAD, T], F32)
+            attn = results.tile([P, count, T], F32, name="attn")
             nc.vector.tensor_tensor(
-                out=attn[:], in0=expd[:], in1=inverse[:].unsqueeze(2).to_broadcast([P, QUAD, T]),
+                out=attn[:], in0=expd[:], in1=inverse[:].unsqueeze(2).to_broadcast([P, count, T]),
                 op=ALU.mult,
             )
-            nc.sync.dma_start(out=out_view[:, QUAD * quad : QUAD * (quad + 1), :], in_=attn[:])
+            nc.sync.dma_start(out=out_view[:, first : first + count, :], in_=attn[:])
 
-        for step in range(N_ROUNDS + 2):
-            if step < N_ROUNDS:
-                previous = None
-                for j in range(ROUND * step, ROUND * (step + 1)):
-                    transpose_first(j)
-                    if previous:
-                        pack(*previous)
-                    previous = ("h1", j)
-                pack(*previous)
-            if step == 0:
-                reorder_a()
-            first_active = 1 <= step <= N_ROUNDS
-            quad, rest = divmod(step - 1 - ROUNDS_IN_QUAD, ROUNDS_IN_QUAD)
-            second_active = quad >= 0 and rest == 0
-            for c in range(ROUND):
-                j = ROUND * (step - 1) + c
-                if first_active:
-                    first_product(j)
-                    if c > 0:
-                        pack("ha", j - 1)
-                if second_active and c == 0:
-                    second_product(quad)
-                    mask_and_shift(quad)
-                if second_active and c == 1:
-                    exponentials(quad)
-            if first_active:
-                pack("ha", ROUND * step - 1)
-            if second_active:
-                normalise_and_store(quad)
+        runs = []
+        for size in RUNS:
+            start = sum(len(run) for run in runs)
+            runs.append(list(range(start, start + size)))
+        next_run = {run[0]: following for run, following in zip(runs, runs[1:])}
+        group_ending_at = {}
+        start = 0
+        for size in GROUPS:
+            group_ending_at[start + size - 1] = (start, size)
+            start += size
+
+        run_of_transposes(runs[0])
+        reorder_a()
+        to_exponentiate = None
+        to_normalise = None
+        for slot in range(N_CHUNKS + 4):
+            if slot in next_run:
+                run_of_transposes(next_run[slot])
+            if slot < N_CHUNKS:
+                first_product(slot)
+            if 0 <= slot - 1 < N_CHUNKS:
+                pack("ha", slot - 1)
+            if to_normalise:
+                normalise_and_store(*to_normalise)
+            to_normalise = to_exponentiate
+            if to_exponentiate:
+                exponentials(*to_exponentiate)
+            to_exponentiate = group_ending_at.get(slot - 2)
+            if to_exponentiate:
+                second_product(*to_exponentiate)
+                mask_and_shift(*to_exponentiate)

@@ -22,8 +22,9 @@ CHUNK = P
 N_CHUNKS = SEQS * T // CHUNK
 SEQS_IN_CHUNK = CHUNK // T
 LOAD = 2
-RUNS = (2, 2) + (4,) * 7
-GROUPS = (4,) * 8
+RUNS = (2,) * 16
+GROUPS = (4,) * 7 + (2, 1, 1)
+WARM_UPS = 10
 NEG_INF = -1e30
 
 assert sum(RUNS) == N_CHUNKS and sum(GROUPS) == N_CHUNKS
@@ -50,12 +51,14 @@ def tile_causalselfattention_pa_t_e_kernel(tc, h, A_words, A_scales, out):
         warm = const.tile([P, 1], F32)
         nc.vector.memset(warm[:], 0.0)
         nc.scalar.activation(out=warm[:], in_=warm[:], func=EXP)
+        idle_rows = const.tile([P, K_PASS], BF16)
+        nc.vector.memset(idle_rows[:], 0.0)
         ident_f32 = const.tile([P, P], F32)
         make_identity(nc, ident_f32[:])
-        mask = const.tile([P, P], F32)
-        nc.gpsimd.memset(mask[:], 0.0)
+        wall = const.tile([P, P], F32)
+        nc.gpsimd.memset(wall[:], 0.0)
         nc.gpsimd.affine_select(
-            out=mask[:], in_=mask[:], compare_op=ALU.is_ge, fill=NEG_INF,
+            out=wall[:], in_=wall[:], compare_op=ALU.is_ge, fill=-NEG_INF,
             base=0, pattern=[[-1, P]], channel_multiplier=1,
         )
 
@@ -175,37 +178,41 @@ def tile_causalselfattention_pa_t_e_kernel(tc, h, A_words, A_scales, out):
                     )
             softmax_tiles[("scores", first)] = scores
 
-        def mask_and_shift(first, count):
+        def mask_and_top(first, count):
             scores = softmax_tiles[("scores", first)]
-            masked = soft.tile([P, count, T], F32, name="masked")
+            flipped = soft.tile([P, count, T], F32, name="flipped")
             for q in range(SEQS_IN_CHUNK):
                 own = slice(T * q, T * (q + 1))
-                nc.vector.tensor_tensor(
-                    out=masked[own, :, :],
+                nc.vector.scalar_tensor_tensor(
+                    out=flipped[own, :, :],
                     in0=scores[own, :, own],
-                    in1=mask[own, own].unsqueeze(1).to_broadcast([T, count, T]),
-                    op=ALU.add,
+                    scalar=-1.0,
+                    in1=wall[own, own].unsqueeze(1).to_broadcast([T, count, T]),
+                    op0=ALU.mult,
+                    op1=ALU.add,
                 )
-            top = soft.tile([P, count], F32, name="top")
-            nc.vector.tensor_reduce(out=top[:], in_=masked[:], axis=LAST_AXIS, op=ALU.max)
-            shifted = soft.tile([P, count, T], F32, name="shifted")
-            nc.vector.tensor_tensor(
-                out=shifted[:], in0=masked[:], in1=top[:].unsqueeze(2).to_broadcast([P, count, T]),
-                op=ALU.subtract,
-            )
-            softmax_tiles[("shifted", first)] = shifted
+            low = soft.tile([P, count], F32, name="low")
+            nc.vector.tensor_reduce(out=low[:], in_=flipped[:], axis=LAST_AXIS, op=ALU.min)
+            softmax_tiles[("flipped", first)] = flipped
+            softmax_tiles[("low", first)] = low
 
         def exponentials(first, count):
+            flipped = softmax_tiles[("flipped", first)]
+            low = softmax_tiles[("low", first)]
             expd = soft.tile([P, count, T], F32, name="expd")
-            nc.scalar.activation(out=expd[:], in_=softmax_tiles[("shifted", first)][:], func=EXP)
+            total = soft.tile([P, count], F32, name="total")
+            for c in range(count):
+                nc.scalar.activation(
+                    out=expd[:, c, :], in_=flipped[:, c, :], func=EXP, scale=-1.0,
+                    bias=low[:, c : c + 1], accum_out=total[:, c : c + 1],
+                )
             softmax_tiles[("expd", first)] = expd
+            softmax_tiles[("total", first)] = total
 
         def normalise_and_store(first, count):
             expd = softmax_tiles[("expd", first)]
-            total = soft.tile([P, count], F32, name="total")
-            nc.vector.tensor_reduce(out=total[:], in_=expd[:], axis=LAST_AXIS, op=ALU.add)
             inverse = soft.tile([P, count], F32, name="inverse")
-            nc.vector.reciprocal(out=inverse[:], in_=total[:])
+            nc.vector.reciprocal(out=inverse[:], in_=softmax_tiles[("total", first)][:])
             attn = results.tile([P, count, T], F32, name="attn")
             nc.vector.tensor_tensor(
                 out=attn[:], in0=expd[:], in1=inverse[:].unsqueeze(2).to_broadcast([P, count, T]),
@@ -231,6 +238,12 @@ def tile_causalselfattention_pa_t_e_kernel(tc, h, A_words, A_scales, out):
         for slot in range(N_CHUNKS + 4):
             if slot in next_run:
                 run_of_transposes(next_run[slot])
+            if slot == 0:
+                idle_sums = mx_psum.tile([P, K_PASS], F32, tag="mx")
+                for i in range(WARM_UPS):
+                    nc.tensor.matmul(
+                        idle_sums[:], lhsT=idle_rows[:, :P], rhs=idle_rows[:], start=True, stop=True
+                    )
             if slot < N_CHUNKS:
                 first_product(slot)
             if 0 <= slot - 1 < N_CHUNKS:
@@ -243,4 +256,4 @@ def tile_causalselfattention_pa_t_e_kernel(tc, h, A_words, A_scales, out):
             to_exponentiate = group_ending_at.get(slot - 2)
             if to_exponentiate:
                 second_product(*to_exponentiate)
-                mask_and_shift(*to_exponentiate)
+                mask_and_top(*to_exponentiate)

@@ -154,10 +154,7 @@ def tile_causalselfattention_pa_t_e_kernel(tc, h, A_words, A_scales, out):
                             start=(gd == 0),
                             stop=(gd == PASSES - 1),
                         )
-                if j % 2 == 1 and ge == PASSES - 1:
-                    nc.vector.tensor_copy(out=ha_values[:, ge], in_=acc[:].rearrange("p t k -> p k t"))
-                else:
-                    nc.scalar.copy(out=ha_values[:, ge], in_=acc[:].rearrange("p t k -> p k t"))
+                nc.scalar.copy(out=ha_values[:, ge], in_=acc[:].rearrange("p t k -> p k t"))
 
         softmax_tiles = {}
 

@@ -24,7 +24,7 @@ SEQS_IN_CHUNK = CHUNK // T
 LOAD = 2
 RUNS = (2,) * 16
 GROUPS = (4,) * 7 + (2, 1, 1)
-WARM_UPS = 10
+WARM_UPS = 6
 NEG_INF = -1e30
 
 assert sum(RUNS) == N_CHUNKS and sum(GROUPS) == N_CHUNKS
@@ -77,10 +77,11 @@ def tile_causalselfattention_pa_t_e_kernel(tc, h, A_words, A_scales, out):
                         out=raw_planes[row:P:32, :, :].bitcast(I32),
                         in_=scale_rows[:, row:16:4, :].rearrange("g q n -> q g n"),
                     )
-                for gd in range(PASSES):
+                for ge in range(PASSES):
+                    half = slice(PACK * K_PASS * ge, PACK * K_PASS * (ge + 1))
                     nc.sync.dma_start(
-                        out=raw_words[:, gd, :].bitcast(I32),
-                        in_=A_words[gd].rearrange("p n t -> p (n t)").bitcast(I32),
+                        out=raw_words[:, :, half].bitcast(I32),
+                        in_=A_words.rearrange("g p n t -> p g (n t)")[:, :, half].bitcast(I32),
                     )
 
         def reorder_a():
@@ -137,24 +138,27 @@ def tile_causalselfattention_pa_t_e_kernel(tc, h, A_words, A_scales, out):
                 previous = j
             pack("h", previous)
 
-        def first_product(j):
+        def first_product_half(j, ge):
             h_words, h_scales = codes[("h", j)]
-            ha_values = new_values("ha", j)
+            ha_values = new_values("ha", j) if ge == 0 else values[("ha", j)]
+            acc = mx_psum.tile([P, PACK, CHUNK], F32, tag="mx")
+            for t in range(PACK):
+                m = PACK * ge + t
+                for gd in range(PASSES):
+                    nc.tensor.matmul_mx(
+                        out=acc[:, t, :],
+                        lhsT=a_words[:, gd, PACK * P * m : PACK * P * (m + 1)].bitcast(FP8X4),
+                        lhsT_scale=a_planes[:, gd, P * m : P * (m + 1)],
+                        rhs=h_words[:, gd, :].bitcast(FP8X4),
+                        rhs_scale=h_scales[:, gd, :],
+                        start=(gd == 0),
+                        stop=(gd == PASSES - 1),
+                    )
+            nc.scalar.copy(out=ha_values[:, ge], in_=acc[:].rearrange("p t k -> p k t"))
+
+        def first_product(j):
             for ge in range(PASSES):
-                acc = mx_psum.tile([P, PACK, CHUNK], F32, tag="mx")
-                for t in range(PACK):
-                    m = PACK * ge + t
-                    for gd in range(PASSES):
-                        nc.tensor.matmul_mx(
-                            out=acc[:, t, :],
-                            lhsT=a_words[:, gd, PACK * P * m : PACK * P * (m + 1)].bitcast(FP8X4),
-                            lhsT_scale=a_planes[:, gd, P * m : P * (m + 1)],
-                            rhs=h_words[:, gd, :].bitcast(FP8X4),
-                            rhs_scale=h_scales[:, gd, :],
-                            start=(gd == 0),
-                            stop=(gd == PASSES - 1),
-                        )
-                nc.scalar.copy(out=ha_values[:, ge], in_=acc[:].rearrange("p t k -> p k t"))
+                first_product_half(j, ge)
 
         softmax_tiles = {}
 
@@ -241,7 +245,10 @@ def tile_causalselfattention_pa_t_e_kernel(tc, h, A_words, A_scales, out):
                     nc.tensor.matmul(
                         idle_sums[:], lhsT=idle_rows[:, :P], rhs=idle_rows[:], start=True, stop=True
                     )
-            if slot < N_CHUNKS:
+                for ge in range(PASSES):
+                    for j in runs[0]:
+                        first_product_half(j, ge)
+            if slot < N_CHUNKS and slot not in runs[0]:
                 first_product(slot)
             if 0 <= slot - 1 < N_CHUNKS:
                 pack("ha", slot - 1)

@@ -24,6 +24,7 @@ SEQS_IN_CHUNK = CHUNK // T
 LOAD = 2
 RUNS = (2,) * 16
 GROUPS = (4,) * 7 + (2, 1, 1)
+PIECES = 2
 WARM_UPS = 6
 NEG_INF = -1e30
 
@@ -92,10 +93,12 @@ def tile_causalselfattention_pa_t_e_kernel(tc, h, A_words, A_scales, out):
                 )
             for ge in range(PASSES):
                 half = slice(K_PASS * ge, K_PASS * (ge + 1))
-                nc.vector.tensor_copy(
-                    out=a_words[:].bitcast(I32)[:, :, half].rearrange("p g (t m) -> p g t m", t=PACK),
-                    in_=raw_words[:].bitcast(I32)[:, :, half].rearrange("p g (m t) -> p g t m", t=PACK),
-                )
+                for piece in range(PIECES):
+                    tiles = slice(PACK // PIECES * piece, PACK // PIECES * (piece + 1))
+                    nc.vector.tensor_copy(
+                        out=a_words[:].bitcast(I32)[:, :, half].rearrange("p g (t m) -> p g t m", t=PACK)[:, :, tiles, :],
+                        in_=raw_words[:].bitcast(I32)[:, :, half].rearrange("p g (m t) -> p g t m", t=PACK)[:, :, tiles, :],
+                    )
 
         out_view = out.rearrange("(c q) o t s -> (q o t) c s", q=SEQS_IN_CHUNK)
 
@@ -138,27 +141,43 @@ def tile_causalselfattention_pa_t_e_kernel(tc, h, A_words, A_scales, out):
                 previous = j
             pack("h", previous)
 
-        def first_product_half(j, ge):
+        def first_product_tile(j, ge, t, acc):
             h_words, h_scales = codes[("h", j)]
+            m = PACK * ge + t
+            for gd in range(PASSES):
+                nc.tensor.matmul_mx(
+                    out=acc[:, t, :],
+                    lhsT=a_words[:, gd, PACK * P * m : PACK * P * (m + 1)].bitcast(FP8X4),
+                    lhsT_scale=a_planes[:, gd, P * m : P * (m + 1)],
+                    rhs=h_words[:, gd, :].bitcast(FP8X4),
+                    rhs_scale=h_scales[:, gd, :],
+                    start=(gd == 0),
+                    stop=(gd == PASSES - 1),
+                )
+
+        def copy_out(j, ge, acc):
             ha_values = new_values("ha", j) if ge == 0 else values[("ha", j)]
-            acc = mx_psum.tile([P, PACK, CHUNK], F32, tag="mx")
-            for t in range(PACK):
-                m = PACK * ge + t
-                for gd in range(PASSES):
-                    nc.tensor.matmul_mx(
-                        out=acc[:, t, :],
-                        lhsT=a_words[:, gd, PACK * P * m : PACK * P * (m + 1)].bitcast(FP8X4),
-                        lhsT_scale=a_planes[:, gd, P * m : P * (m + 1)],
-                        rhs=h_words[:, gd, :].bitcast(FP8X4),
-                        rhs_scale=h_scales[:, gd, :],
-                        start=(gd == 0),
-                        stop=(gd == PASSES - 1),
-                    )
             nc.scalar.copy(out=ha_values[:, ge], in_=acc[:].rearrange("p t k -> p k t"))
 
         def first_product(j):
             for ge in range(PASSES):
-                first_product_half(j, ge)
+                acc = mx_psum.tile([P, PACK, CHUNK], F32, tag="mx")
+                for t in range(PACK):
+                    first_product_tile(j, ge, t, acc)
+                copy_out(j, ge, acc)
+
+        def first_product_of_first_run(chunks):
+            for ge in range(PASSES):
+                banks = []
+                for j in chunks:
+                    acc = mx_psum.tile([P, PACK, CHUNK], F32, tag="mx")
+                    banks.append(acc)
+                for piece in range(PIECES):
+                    for j, acc in zip(chunks, banks):
+                        for t in range(PACK // PIECES * piece, PACK // PIECES * (piece + 1)):
+                            first_product_tile(j, ge, t, acc)
+                for j, acc in zip(chunks, banks):
+                    copy_out(j, ge, acc)
 
         softmax_tiles = {}
 
@@ -245,9 +264,7 @@ def tile_causalselfattention_pa_t_e_kernel(tc, h, A_words, A_scales, out):
                     nc.tensor.matmul(
                         idle_sums[:], lhsT=idle_rows[:, :P], rhs=idle_rows[:], start=True, stop=True
                     )
-                for ge in range(PASSES):
-                    for j in runs[0]:
-                        first_product_half(j, ge)
+                first_product_of_first_run(runs[0])
             if slot < N_CHUNKS and slot not in runs[0]:
                 first_product(slot)
             if 0 <= slot - 1 < N_CHUNKS:

from contextlib import ExitStack

import concourse.mybir as mybir
from concourse.masks import make_identity

F32 = mybir.dt.float32
BF16 = mybir.dt.bfloat16
I32 = mybir.dt.int32
U32 = mybir.dt.uint32
U8 = mybir.dt.uint8
FP8X4 = mybir.dt.float8_e4m3fn_x4
ALU = mybir.AluOpType
EXP = mybir.ActivationFunctionType.Exp
LAST_AXIS = mybir.AxisListType.X

P = 128
PACK = 4
K_PASS = P * PACK
SEQS, T, D = 128, 32, 1024
PASSES = D // K_PASS
CHUNK = P
N_CHUNKS = SEQS * T // CHUNK
SEQS_IN_CHUNK = CHUNK // T
LOAD = 2
RUNS = (2,) * 16
GROUPS = (4,) * 7 + (2, 1, 1)
PIECES = 2
WARM_UPS = 6
NEG_INF = -1e30

assert sum(RUNS) == N_CHUNKS and sum(GROUPS) == N_CHUNKS

FLOPS = 2 * SEQS * (T - 1) * D * D + 2 * SEQS * (T - 1) * T * D


def tile_causalselfattention_pa_t_e_kernel(tc, h, A_words, A_scales, out):
    nc = tc.nc
    with ExitStack() as stack:
        stack.enter_context(tc.manual_schedule())
        const = stack.enter_context(tc.tile_pool(name="const", bufs=1))
        h_pool = stack.enter_context(tc.tile_pool(name="h_pool", bufs=N_CHUNKS // LOAD))
        grouped = stack.enter_context(tc.tile_pool(name="grouped", bufs=3))
        packed = stack.enter_context(tc.tile_pool(name="packed", bufs=2 * max(RUNS) + 4))
        soft = stack.enter_context(tc.tile_pool(name="soft", bufs=2))
        results = stack.enter_context(tc.tile_pool(name="results", bufs=len(GROUPS)))
        tp_psum = stack.enter_context(tc.psum_pool(name="tp_psum", bufs=4))
        mx_psum = stack.enter_context(tc.psum_pool(name="mx_psum", bufs=4))

        raw_planes = const.tile([P, PASSES, D], U8, align_bytes=64)
        nc.vector.memset(raw_planes[:].rearrange("p g n -> p (g n)").bitcast(I32), 0)
        a_planes = const.tile([P, PASSES, D], U8, align_bytes=64)
        warm = const.tile([P, 1], F32)
        nc.vector.memset(warm[:], 0.0)
        nc.scalar.activation(out=warm[:], in_=warm[:], func=EXP)
        idle_rows = const.tile([P, K_PASS], BF16)
        nc.vector.memset(idle_rows[:], 0.0)
        ident_f32 = const.tile([P, P], F32)
        make_identity(nc, ident_f32[:])
        wall = const.tile([P, P], F32)
        nc.gpsimd.memset(wall[:], 0.0)
        nc.gpsimd.affine_select(
            out=wall[:], in_=wall[:], compare_op=ALU.is_ge, fill=-NEG_INF,
            base=0, pattern=[[-1, P]], channel_multiplier=1,
        )

        h_loads = h.flatten_outer_dims().rearrange("(r c p) f -> r p c f", c=LOAD, p=P)
        raw_words = const.tile([P, PASSES, PACK * D], U8, align_bytes=64)
        a_words = const.tile([P, PASSES, PACK * D], U8, align_bytes=64)
        scale_rows = A_scales.bitcast(I32)
        h_tiles = []
        for r in range(N_CHUNKS // LOAD):
            h_sb = h_pool.tile([P, LOAD, D], BF16)
            nc.sync.dma_start(out=h_sb[:], in_=h_loads[r])
            h_tiles.append(h_sb)
            if r == 1:
                for row in range(4):
                    nc.sync.dma_start(
                        out=raw_planes[row:P:32, :, :].bitcast(I32),
                        in_=scale_rows[:, row:16:4, :].rearrange("g q n -> q g n"),
                    )
                for ge in range(PASSES):
                    half = slice(PACK * K_PASS * ge, PACK * K_PASS * (ge + 1))
                    nc.sync.dma_start(
                        out=raw_words[:, :, half].bitcast(I32),
                        in_=A_words.rearrange("g p n t -> p g (n t)")[:, :, half].bitcast(I32),
                    )

        def reorder_a():
            for t in range(PACK):
                nc.vector.tensor_copy(
                    out=a_planes[:].rearrange("p g (e t m) -> p t g e m", e=PASSES, t=PACK)[:, t],
                    in_=raw_planes[:].rearrange("p g (e m t) -> p t g e m", e=PASSES, t=PACK)[:, t],
                )
            for ge in range(PASSES):
                half = slice(K_PASS * ge, K_PASS * (ge + 1))
                for piece in range(PIECES):
                    tiles = slice(PACK // PIECES * piece, PACK // PIECES * (piece + 1))
                    nc.vector.tensor_copy(
                        out=a_words[:].bitcast(I32)[:, :, half].rearrange("p g (t m) -> p g t m", t=PACK)[:, :, tiles, :],
                        in_=raw_words[:].bitcast(I32)[:, :, half].rearrange("p g (m t) -> p g t m", t=PACK)[:, :, tiles, :],
                    )

        out_view = out.rearrange("(c q) o t s -> (q o t) c s", q=SEQS_IN_CHUNK)

        values = {}
        codes = {}

        def new_values(kind, j):
            fresh = grouped.tile([P, PASSES, CHUNK, PACK], BF16, align_bytes=64, name=kind + "_values")
            values[(kind, j)] = fresh
            return fresh

        def pack(kind, j):
            words = packed.tile([P, PASSES, CHUNK], U32, align_bytes=64, name=kind + "_words")
            scales = packed.tile([P, PASSES, CHUNK], U8, align_bytes=64, name=kind + "_scales")
            nc.vector.quantize_mx(
                out=words[:].rearrange("p g k -> p (g k)").bitcast(FP8X4),
                scales=scales[:].rearrange("p g k -> p (g k)"),
                in_=values[(kind, j)][:].rearrange("p g k t -> p (g k t)"),
            )
            codes[(kind, j)] = (words, scales)

        def transposes(j):
            pairs = h_tiles[j // LOAD][:, j % LOAD, :].bitcast(F32)
            tp = tp_psum.tile([P, PASSES, 2, CHUNK], F32, tag="tp")
            for g in range(PASSES):
                for u in range(2):
                    nc.tensor.transpose(
                        tp[:, g, u, :], pairs[:, 256 * g + u : 256 * (g + 1) : 2], ident_f32[:]
                    )
            nc.scalar.copy(
                out=new_values("h", j)[:].bitcast(F32), in_=tp[:].rearrange("p g u k -> p g k u")
            )

        def run_of_transposes(chunks):
            previous = None
            for j in chunks:
                transposes(j)
                if previous is not None:
                    pack("h", previous)
                previous = j
            pack("h", previous)

        def first_product_tile(j, ge, t, acc):
            h_words, h_scales = codes[("h", j)]
            m = PACK * ge + t
            for gd in range(PASSES):
                nc.tensor.matmul_mx(
                    out=acc[:, t, :],
                    lhsT=a_words[:, gd, PACK * P * m : PACK * P * (m + 1)].bitcast(FP8X4),
                    lhsT_scale=a_planes[:, gd, P * m : P * (m + 1)],
                    rhs=h_words[:, gd, :].bitcast(FP8X4),
                    rhs_scale=h_scales[:, gd, :],
                    start=(gd == 0),
                    stop=(gd == PASSES - 1),
                )

        def copy_out(j, ge, acc):
            ha_values = new_values("ha", j) if ge == 0 else values[("ha", j)]
            nc.scalar.copy(out=ha_values[:, ge], in_=acc[:].rearrange("p t k -> p k t"))

        def first_product(j):
            for ge in range(PASSES):
                acc = mx_psum.tile([P, PACK, CHUNK], F32, tag="mx")
                for t in range(PACK):
                    first_product_tile(j, ge, t, acc)
                copy_out(j, ge, acc)

        def first_product_of_first_run(chunks):
            for ge in range(PASSES):
                banks = []
                for j in chunks:
                    acc = mx_psum.tile([P, PACK, CHUNK], F32, tag="mx")
                    banks.append(acc)
                for piece in range(PIECES):
                    for j, acc in zip(chunks, banks):
                        for t in range(PACK // PIECES * piece, PACK // PIECES * (piece + 1)):
                            first_product_tile(j, ge, t, acc)
                for j, acc in zip(chunks, banks):
                    copy_out(j, ge, acc)

        softmax_tiles = {}

        def second_product(first, count):
            scores = mx_psum.tile([P, count, CHUNK], F32, tag="mx")
            for c in range(count):
                ha_words, ha_scales = codes[("ha", first + c)]
                h_words, h_scales = codes[("h", first + c)]
                for ge in range(PASSES):
                    nc.tensor.matmul_mx(
                        out=scores[:, c, :],
                        lhsT=ha_words[:, ge, :].bitcast(FP8X4),
                        lhsT_scale=ha_scales[:, ge, :],
                        rhs=h_words[:, ge, :].bitcast(FP8X4),
                        rhs_scale=h_scales[:, ge, :],
                        start=(ge == 0),
                        stop=(ge == PASSES - 1),
                    )
            softmax_tiles[("scores", first)] = scores

        def mask_and_top(first, count):
            scores = softmax_tiles[("scores", first)]
            flipped = soft.tile([P, count, T], F32, name="flipped")
            for q in range(SEQS_IN_CHUNK):
                own = slice(T * q, T * (q + 1))
                nc.vector.scalar_tensor_tensor(
                    out=flipped[own, :, :],
                    in0=scores[own, :, own],
                    scalar=-1.0,
                    in1=wall[own, own].unsqueeze(1).to_broadcast([T, count, T]),
                    op0=ALU.mult,
                    op1=ALU.add,
                )
            low = soft.tile([P, count], F32, name="low")
            nc.vector.tensor_reduce(out=low[:], in_=flipped[:], axis=LAST_AXIS, op=ALU.min)
            softmax_tiles[("flipped", first)] = flipped
            softmax_tiles[("low", first)] = low

        def exponentials(first, count):
            flipped = softmax_tiles[("flipped", first)]
            low = softmax_tiles[("low", first)]
            expd = soft.tile([P, count, T], F32, name="expd")
            total = soft.tile([P, count], F32, name="total")
            for c in range(count):
                nc.scalar.activation(
                    out=expd[:, c, :], in_=flipped[:, c, :], func=EXP, scale=-1.0,
                    bias=low[:, c : c + 1], accum_out=total[:, c : c + 1],
                )
            softmax_tiles[("expd", first)] = expd
            softmax_tiles[("total", first)] = total

        def normalise_and_store(first, count):
            expd = softmax_tiles[("expd", first)]
            inverse = soft.tile([P, count], F32, name="inverse")
            nc.vector.reciprocal(out=inverse[:], in_=softmax_tiles[("total", first)][:])
            attn = results.tile([P, count, T], F32, name="attn")
            nc.vector.tensor_tensor(
                out=attn[:], in0=expd[:], in1=inverse[:].unsqueeze(2).to_broadcast([P, count, T]),
                op=ALU.mult,
            )
            nc.sync.dma_start(out=out_view[:, first : first + count, :], in_=attn[:])

        runs = []
        for size in RUNS:
            start = sum(len(run) for run in runs)
            runs.append(list(range(start, start + size)))
        next_run = {run[0]: following for run, following in zip(runs, runs[1:])}
        group_ending_at = {}
        start = 0
        for size in GROUPS:
            group_ending_at[start + size - 1] = (start, size)
            start += size

        run_of_transposes(runs[0])
        reorder_a()
        to_exponentiate = None
        to_normalise = None
        for slot in range(N_CHUNKS + 4):
            if slot in next_run:
                run_of_transposes(next_run[slot])
            if slot == 0:
                idle_sums = mx_psum.tile([P, K_PASS], F32, tag="mx")
                for i in range(WARM_UPS):
                    nc.tensor.matmul(
                        idle_sums[:], lhsT=idle_rows[:, :P], rhs=idle_rows[:], start=True, stop=True
                    )
                first_product_of_first_run(runs[0])
            if slot < N_CHUNKS and slot not in runs[0]:
                first_product(slot)
            if 0 <= slot - 1 < N_CHUNKS:
                pack("ha", slot - 1)
            if to_normalise:
                normalise_and_store(*to_normalise)
            to_normalise = to_exponentiate
            if to_exponentiate:
                exponentials(*to_exponentiate)
            to_exponentiate = group_ending_at.get(slot - 2)
            if to_exponentiate:
                second_product(*to_exponentiate)
                mask_and_top(*to_exponentiate)
